import numpy as np
import ml_dtypes


def mxq(x, axis, fmt="e4m3"):
    dtype, down = {"e4m3": (ml_dtypes.float8_e4m3fn, 7), "e5m2": (ml_dtypes.float8_e5m2, 14)}[fmt]
    v = np.moveaxis(np.asarray(x, np.float32).astype(ml_dtypes.bfloat16).astype(np.float64), axis, -1)
    blocks = v.reshape(v.shape[:-1] + (-1, 32))
    amax = np.abs(blocks).max(-1, keepdims=True)
    byte = np.maximum(np.where(amax > 0, np.frexp(amax)[1] - 1 + 127, 0) - down, 1)
    scale = np.exp2(byte - 127.0)
    codes = (blocks / scale).astype(np.float32).astype(dtype).astype(np.float64)
    return np.moveaxis((codes * scale).reshape(v.shape), -1, axis)


WIDE = False


def mx_kscale(k):
    if not WIDE:
        return np.ones(k)
    levels = np.array([10, -10, 5, -5, 0])
    a = np.random.permutation(np.resize(levels, k // 512 * 4)).reshape(k // 512, 4)
    idx = np.arange(k)
    return np.exp2(a[idx // 512, idx % 128 // 32])


BF16 = ml_dtypes.bfloat16


def bf(x):
    return np.asarray(x, np.float32).astype(BF16)


def f64(x):
    return np.asarray(x).astype(np.float64)


H, D_CONTENT, D_POS, D_K, D_V, B, L = 8, 768, 256, 128, 128, 4, 256
D_MODEL = D_CONTENT + D_POS
T = B * L
DV1 = D_V // 2
KP = H * DV1
EPS = 1e-3


def setup_inputs():
    s1, s2 = mx_kscale(KP), mx_kscale(KP)
    sc = np.concatenate([s1.reshape(H, DV1), s2.reshape(H, DV1)], axis=1)
    return {
        "attn_out": bf(np.random.standard_normal((H, B, L, D_V)) * 0.4 * sc[:, None, None, :]),
        "inp": bf(np.random.standard_normal((T, D_MODEL)) * 0.05 + np.random.standard_normal((T, 1)) * 0.03),
        "w_proj1": bf(np.random.standard_normal((KP, D_CONTENT)) * 0.1 / np.sqrt(KP) / s1[:, None]),
        "w_proj2": bf(np.random.standard_normal((KP, D_POS)) * 0.1 / np.sqrt(KP) / s2[:, None]),
        "ln_a": bf(1.0 + 0.1 * np.random.standard_normal(D_MODEL)),
        "ln_b": bf(0.1 * np.random.standard_normal(D_MODEL)),
    }


def reference(attn_out, inp, w_proj1, w_proj2, ln_a, ln_b):
    o = f64(attn_out).reshape(H, T, D_V).transpose(1, 0, 2)
    o1 = o[:, :, :DV1].reshape(T, KP)
    o2 = o[:, :, DV1:].reshape(T, KP)
    y1 = mxq(o1, 1, "e4m3") @ mxq(f64(w_proj1), 0, "e4m3")
    y2 = mxq(o2, 1, "e4m3") @ mxq(f64(w_proj2), 0, "e4m3")
    z = np.concatenate([y1, y2], -1) + f64(inp)
    mu = np.mean(z, axis=-1, keepdims=True)
    sigma = np.std(z, axis=-1, keepdims=True, ddof=1)
    ln = (z - mu) / (sigma + EPS)
    return ln * f64(ln_a) + f64(ln_b)

@@ -1,0 +1,208 @@
+from contextlib import ExitStack
+
+import concourse.mybir as mybir
+from concourse.masks import make_identity
+
+F32 = mybir.dt.float32
+BF16 = mybir.dt.bfloat16
+U32 = mybir.dt.uint32
+U8 = mybir.dt.uint8
+FP8X4 = mybir.dt.float8_e4m3fn_x4
+ALU = mybir.AluOpType
+ACT = mybir.ActivationFunctionType
+
+P = 128
+HEADS = 8
+D_V = 128
+HALF = D_V // 2
+TOKENS = 1024
+K = HEADS * HALF
+N1 = 768
+N2 = 256
+D_MODEL = N1 + N2
+BANK = 512
+EPS = 1e-3
+TINY = 1e-30
+
+ROWS = 2
+GROUPS = TOKENS // (P * ROWS)
+
+FLOPS = 2 * TOKENS * K * D_MODEL
+
+
+def tile_multiheadattention_pa_kernel(tc, attn_out, inp, w_proj1, w_proj2, ln_a, ln_b, out):
+    nc = tc.nc
+    attn_groups = attn_out.rearrange("h g (p r) d -> g p h (r d)", r=ROWS)
+    inp_groups = inp.rearrange("(g p r) n -> g p (r n)", g=GROUPS, r=ROWS)
+    out_groups = out.rearrange("(g p r) n -> g p r n", g=GROUPS, r=ROWS)
+
+    with ExitStack() as ctx:
+        keep = ctx.enter_context(tc.tile_pool(name="keep", bufs=1))
+        loads = ctx.enter_context(tc.tile_pool(name="loads", bufs=GROUPS))
+        stage = ctx.enter_context(tc.tile_pool(name="stage", bufs=3))
+        work = ctx.enter_context(tc.tile_pool(name="work", bufs=3))
+        small = ctx.enter_context(tc.tile_pool(name="small", bufs=4))
+        gain_psum = ctx.enter_context(tc.psum_pool(name="gain_psum", bufs=1))
+        y_psum = ctx.enter_context(tc.psum_pool(name="y_psum", bufs=2))
+        t_psum = ctx.enter_context(tc.psum_pool(name="t_psum", bufs=2))
+
+        one = keep.tile([P, 1], F32)
+        nc.vector.memset(one[:], 1.0)
+        warm = keep.tile([P, 1], F32)
+        nc.scalar.activation(out=warm[:], in_=one[:], func=ACT.Sqrt)
+
+        ident = keep.tile([P, P], F32)
+        make_identity(nc, ident[:])
+        ones = keep.tile([P, P], BF16)
+        nc.vector.memset(ones[:], 1.0)
+        rows = keep.tile([P, 2 * D_MODEL], BF16)
+        nc.vector.memset(rows[:], 0.0)
+
+        x_raw = []
+        inp_sb = []
+
+        def load_group(g):
+            x_g = loads.tile([P, HEADS, ROWS * D_V], BF16, name="x_raw")
+            nc.sync.dma_start(out=x_g[:], in_=attn_groups[g])
+            x_raw.append(x_g)
+
+        def load_residual(g):
+            inp_g = loads.tile([P, ROWS, D_MODEL], BF16, name="inp_sb")
+            nc.sync.dma_start(out=inp_g[:].rearrange("p r n -> p (r n)"), in_=inp_groups[g])
+            inp_sb.append(inp_g)
+
+        load_group(0)
+        w2_raw = keep.tile([P, 4, N2], BF16)
+        nc.sync.dma_start(
+            out=w2_raw[:].rearrange("q (u e) n -> q u (e n)", u=2), in_=w_proj2.rearrange("(u q e) n -> q u (e n)", u=2, e=2)
+        )
+        w1_raw = keep.tile([P, 4, N1], BF16)
+        nc.sync.dma_start(
+            out=w1_raw[:].rearrange("q (u e) n -> q u (e n)", u=2), in_=w_proj1.rearrange("(u q e) n -> q u (e n)", u=2, e=2)
+        )
+        load_residual(0)
+        nc.sync.dma_start(out=rows[0:1, 0:D_MODEL], in_=ln_a.unsqueeze(0))
+        nc.sync.dma_start(out=rows[0:1, D_MODEL : 2 * D_MODEL], in_=ln_b.unsqueeze(0))
+        for g in range(1, GROUPS):
+            load_group(g)
+            load_residual(g)
+
+        w_grouped = keep.tile([P, D_MODEL, 4], BF16, align_bytes=64)
+        w_codes = keep.tile([P, D_MODEL], U32, align_bytes=64)
+        w_scales = keep.tile([P, D_MODEL], U8, align_bytes=64)
+
+        def regroup(copy, first, raw_cols):
+            width = raw_cols.shape[2]
+            copy(
+                out=w_grouped[:, first : first + width, :].rearrange("p (c i) t -> p c t i", i=4),
+                in_=raw_cols.rearrange("p t (c i) -> p c t i", i=4),
+            )
+
+        regroup(nc.scalar.copy, N1, w2_raw[:])
+        regroup(nc.vector.tensor_copy, 0, w1_raw[:, :, 0:BANK])
+        regroup(nc.scalar.copy, BANK, w1_raw[:, :, BANK:N1])
+        for c in range(2):
+            cols = slice(c * BANK, (c + 1) * BANK)
+            nc.vector.quantize_mx(
+                out=w_codes[:, cols].bitcast(FP8X4),
+                scales=w_scales[:, cols],
+                in_=w_grouped[:, cols, :].rearrange("p n t -> p (n t)"),
+            )
+
+        o_codes = keep.tile([P, GROUPS * ROWS, 2 * P], U32, align_bytes=64)
+        o_scales = keep.tile([P, GROUPS * ROWS, 2 * P], U8, align_bytes=64)
+
+        def quantise_group(g):
+            x_split = stage.tile([P, ROWS, 2, K], BF16)
+            nc.vector.tensor_copy(
+                out=x_split[:].rearrange("p r s (h j) -> p r s h j", j=HALF),
+                in_=x_raw[g][:].rearrange("p h (r s j) -> p r s h j", r=ROWS, s=2),
+            )
+            x_words = x_split[:].bitcast(F32)
+            for r in range(ROWS):
+                xt = t_psum.tile([P, 2, 2, P], F32, tag="xt")
+                for s in range(2):
+                    for u in range(2):
+                        nc.tensor.transpose(xt[:, s, u, :], x_words[:, r, s, u * P : (u + 1) * P], ident[:])
+                grouped = stage.tile([P, 2, P, 4], BF16, align_bytes=64)
+                nc.scalar.copy(out=grouped[:].bitcast(F32), in_=xt[:].rearrange("p s u m -> p s m u"))
+                nc.vector.quantize_mx(
+                    out=o_codes[:, g * ROWS + r, :].bitcast(FP8X4),
+                    scales=o_scales[:, g * ROWS + r, :],
+                    in_=grouped[:].rearrange("p s m t -> p (s m t)"),
+                )
+
+        def project(tile_index):
+            def mx(acc, s, cols):
+                nc.tensor.matmul_mx(
+                    out=acc,
+                    lhsT=o_codes[:, tile_index, s * P : (s + 1) * P].bitcast(FP8X4),
+                    lhsT_scale=o_scales[:, tile_index, s * P : (s + 1) * P],
+                    rhs=w_codes[:, cols].bitcast(FP8X4),
+                    rhs_scale=w_scales[:, cols],
+                    start=True,
+                    stop=True,
+                )
+
+            y0 = y_psum.tile([P, BANK], F32)
+            y1 = y_psum.tile([P, BANK], F32)
+            mx(y0[:], 0, slice(0, BANK))
+            mx(y1[:, 0 : N1 - BANK], 0, slice(BANK, N1))
+            mx(y1[:, N1 - BANK : BANK], 1, slice(N1, D_MODEL))
+            return [y0, y1]
+
+        def norm(g, r, y):
+            z = work.tile([P, D_MODEL], F32)
+            sums = small.tile([P, 2], F32)
+            for c in range(2):
+                cols = slice(c * BANK, (c + 1) * BANK)
+                nc.vector.scalar_tensor_tensor(
+                    out=z[:, cols], in0=y[c][:], scalar=1.0, in1=inp_sb[g][:, r, cols],
+                    op0=ALU.mult, op1=ALU.add, accum_out=sums[:, c : c + 1],
+                )
+            neg_mean = small.tile([P, 1], F32)
+            nc.vector.tensor_scalar(
+                out=neg_mean[:], in0=sums[:, 0:1], scalar1=sums[:, 1:2], scalar2=-1.0 / D_MODEL, op0=ALU.add, op1=ALU.mult
+            )
+            squares = work.tile([P, D_MODEL], BF16)
+            sum_sq = small.tile([P, 1], F32)
+            nc.scalar.activation(out=squares[:], in_=z[:], func=ACT.Square, bias=neg_mean[:], scale=1.0, accum_out=sum_sq[:])
+            sigma = small.tile([P, 1], F32)
+            nc.scalar.activation(out=sigma[:], in_=sum_sq[:], func=ACT.Sqrt, bias=TINY, scale=1.0 / (D_MODEL - 1))
+            gained = work.tile([P, D_MODEL], F32)
+            for c in range(2):
+                cols = slice(c * BANK, (c + 1) * BANK)
+                nc.vector.scalar_tensor_tensor(
+                    out=gained[:, cols], in0=z[:, cols], scalar=neg_mean[:], in1=gain[c][:], op0=ALU.add, op1=ALU.mult
+                )
+            denom = small.tile([P, 1], F32)
+            nc.vector.tensor_scalar_add(out=denom[:], in0=sigma[:], scalar1=EPS)
+            inv = small.tile([P, 1], F32)
+            nc.vector.reciprocal(out=inv[:], in_=denom[:])
+            scaled = work.tile([P, D_MODEL], F32)
+            nc.scalar.activation(out=scaled[:], in_=gained[:], func=ACT.Copy, scale=inv[:])
+            result = work.tile([P, D_MODEL], F32)
+            nc.gpsimd.tensor_tensor(out=result[:], in0=scaled[:], in1=bias[:], op=ALU.add)
+            nc.sync.dma_start(out=out_groups[g][:, r, :], in_=result[:])
+
+        quantise_group(0)
+        first = [project(r) for r in range(ROWS)]
+
+        gain = []
+        for c in range(2):
+            gain_c = gain_psum.tile([P, BANK], F32, name="gain%d" % c)
+            nc.tensor.matmul(out=gain_c[:], lhsT=ones[:], rhs=rows[:, c * BANK : (c + 1) * BANK], start=True, stop=True)
+            gain.append(gain_c)
+        bias = keep.tile([P, D_MODEL], F32)
+        for c in range(2):
+            bias_c = t_psum.tile([P, BANK], F32, tag="xt")
+            nc.tensor.matmul(
+                out=bias_c[:], lhsT=ones[:], rhs=rows[:, D_MODEL + c * BANK : D_MODEL + (c + 1) * BANK], start=True, stop=True
+            )
+            nc.scalar.copy(out=bias[:, c * BANK : (c + 1) * BANK], in_=bias_c[:])
+
+        for g in range(GROUPS):
+            if g + 1 < GROUPS:
+                quantise_group(g + 1)
+            for r in range(ROWS):
+                norm(g, r, first[r] if g == 0 else project(g * ROWS + r))

@@ -26,6 +26,11 @@ TINY = 1e-30
 
 ROWS = 2
 GROUPS = TOKENS // (P * ROWS)
+TILES = GROUPS * ROWS
+
+TAIL_TILES = 2
+G_FIRST = 768
+TAIL_V_COLS = 768
 
 FLOPS = 2 * TOKENS * K * D_MODEL
 
@@ -45,23 +50,23 @@ def tile_multiheadattention_pa_kernel(tc, attn_out, inp, w_proj1, w_proj2, ln_a,
         gain_psum = ctx.enter_context(tc.psum_pool(name="gain_psum", bufs=1))
         y_psum = ctx.enter_context(tc.psum_pool(name="y_psum", bufs=2))
         t_psum = ctx.enter_context(tc.psum_pool(name="t_psum", bufs=2))
+        ctx.enter_context(tc.manual_schedule())
 
+        rows = keep.tile([P, 2 * D_MODEL], BF16)
+        nc.vector.memset(rows[:], 0.0)
+        ones = keep.tile([P, P], BF16)
+        nc.vector.memset(ones[:], 1.0)
         one = keep.tile([P, 1], F32)
         nc.vector.memset(one[:], 1.0)
         warm = keep.tile([P, 1], F32)
         nc.scalar.activation(out=warm[:], in_=one[:], func=ACT.Sqrt)
-
         ident = keep.tile([P, P], F32)
         make_identity(nc, ident[:])
-        ones = keep.tile([P, P], BF16)
-        nc.vector.memset(ones[:], 1.0)
-        rows = keep.tile([P, 2 * D_MODEL], BF16)
-        nc.vector.memset(rows[:], 0.0)
 
         x_raw = []
         inp_sb = []
 
-        def load_group(g):
+        def load_attention(g):
             x_g = loads.tile([P, HEADS, ROWS * D_V], BF16, name="x_raw")
             nc.sync.dma_start(out=x_g[:], in_=attn_groups[g])
             x_raw.append(x_g)
@@ -71,7 +76,9 @@ def tile_multiheadattention_pa_kernel(tc, attn_out, inp, w_proj1, w_proj2, ln_a,
             nc.sync.dma_start(out=inp_g[:].rearrange("p r n -> p (r n)"), in_=inp_groups[g])
             inp_sb.append(inp_g)
 
-        load_group(0)
+        load_attention(0)
+        nc.sync.dma_start(out=rows[0:1, 0:D_MODEL], in_=ln_a.unsqueeze(0))
+        nc.sync.dma_start(out=rows[0:1, D_MODEL : 2 * D_MODEL], in_=ln_b.unsqueeze(0))
         w2_raw = keep.tile([P, 4, N2], BF16)
         nc.sync.dma_start(
             out=w2_raw[:].rearrange("q (u e) n -> q u (e n)", u=2), in_=w_proj2.rearrange("(u q e) n -> q u (e n)", u=2, e=2)
@@ -81,27 +88,22 @@ def tile_multiheadattention_pa_kernel(tc, attn_out, inp, w_proj1, w_proj2, ln_a,
             out=w1_raw[:].rearrange("q (u e) n -> q u (e n)", u=2), in_=w_proj1.rearrange("(u q e) n -> q u (e n)", u=2, e=2)
         )
         load_residual(0)
-        nc.sync.dma_start(out=rows[0:1, 0:D_MODEL], in_=ln_a.unsqueeze(0))
-        nc.sync.dma_start(out=rows[0:1, D_MODEL : 2 * D_MODEL], in_=ln_b.unsqueeze(0))
         for g in range(1, GROUPS):
-            load_group(g)
+            load_attention(g)
             load_residual(g)
 
         w_grouped = keep.tile([P, D_MODEL, 4], BF16, align_bytes=64)
         w_codes = keep.tile([P, D_MODEL], U32, align_bytes=64)
         w_scales = keep.tile([P, D_MODEL], U8, align_bytes=64)
 
-        def regroup(copy, first, raw_cols):
+        def regroup_weight(copy, first, raw_cols):
             width = raw_cols.shape[2]
             copy(
                 out=w_grouped[:, first : first + width, :].rearrange("p (c i) t -> p c t i", i=4),
                 in_=raw_cols.rearrange("p t (c i) -> p c t i", i=4),
             )
 
-        regroup(nc.scalar.copy, N1, w2_raw[:])
-        regroup(nc.vector.tensor_copy, 0, w1_raw[:, :, 0:BANK])
-        regroup(nc.scalar.copy, BANK, w1_raw[:, :, BANK:N1])
-        for c in range(2):
+        def quantise_weight(c):
             cols = slice(c * BANK, (c + 1) * BANK)
             nc.vector.quantize_mx(
                 out=w_codes[:, cols].bitcast(FP8X4),
@@ -109,35 +111,57 @@ def tile_multiheadattention_pa_kernel(tc, attn_out, inp, w_proj1, w_proj2, ln_a,
                 in_=w_grouped[:, cols, :].rearrange("p n t -> p (n t)"),
             )
 
-        o_codes = keep.tile([P, GROUPS * ROWS, 2 * P], U32, align_bytes=64)
-        o_scales = keep.tile([P, GROUPS * ROWS, 2 * P], U8, align_bytes=64)
+        o_codes = keep.tile([P, TILES, 2 * P], U32, align_bytes=64)
+        o_scales = keep.tile([P, TILES, 2 * P], U8, align_bytes=64)
+        x_split = {}
+        xt = {}
+        grouped = {}
+        y = {}
+        z = {}
+        sums = {}
+        neg_mean = {}
+        sum_sq = {}
+        sigma = {}
+        gained = {}
+        denom = {}
+        inv = {}
 
-        def quantise_group(g):
-            x_split = stage.tile([P, ROWS, 2, K], BF16)
+        def sort_features(k):
+            if k % ROWS != 0:
+                return
+            split = stage.tile([P, ROWS, 2, K], BF16, name="x_split")
             nc.vector.tensor_copy(
-                out=x_split[:].rearrange("p r s (h j) -> p r s h j", j=HALF),
-                in_=x_raw[g][:].rearrange("p h (r s j) -> p r s h j", r=ROWS, s=2),
+                out=split[:].rearrange("p r s (h j) -> p r s h j", j=HALF),
+                in_=x_raw[k // ROWS][:].rearrange("p h (r s j) -> p r s h j", r=ROWS, s=2),
             )
-            x_words = x_split[:].bitcast(F32)
-            for r in range(ROWS):
-                xt = t_psum.tile([P, 2, 2, P], F32, tag="xt")
-                for s in range(2):
-                    for u in range(2):
-                        nc.tensor.transpose(xt[:, s, u, :], x_words[:, r, s, u * P : (u + 1) * P], ident[:])
-                grouped = stage.tile([P, 2, P, 4], BF16, align_bytes=64)
-                nc.scalar.copy(out=grouped[:].bitcast(F32), in_=xt[:].rearrange("p s u m -> p s m u"))
-                nc.vector.quantize_mx(
-                    out=o_codes[:, g * ROWS + r, :].bitcast(FP8X4),
-                    scales=o_scales[:, g * ROWS + r, :],
-                    in_=grouped[:].rearrange("p s m t -> p (s m t)"),
-                )
+            x_split[k // ROWS] = split
 
-        def project(tile_index):
+        def flip(k):
+            words = x_split[k // ROWS][:].bitcast(F32)
+            planes = t_psum.tile([P, 2, 2, P], F32, name="xt")
+            for s in range(2):
+                for u in range(2):
+                    nc.tensor.transpose(planes[:, s, u, :], words[:, k % ROWS, s, u * P : (u + 1) * P], ident[:])
+            xt[k] = planes
+
+        def evacuate(k):
+            packed = stage.tile([P, 2, P, 4], BF16, align_bytes=64, name="grouped")
+            nc.scalar.copy(out=packed[:].bitcast(F32), in_=xt[k][:].rearrange("p s u m -> p s m u"))
+            grouped[k] = packed
+
+        def quantise(k):
+            nc.vector.quantize_mx(
+                out=o_codes[:, k, :].bitcast(FP8X4),
+                scales=o_scales[:, k, :],
+                in_=grouped[k][:].rearrange("p s m t -> p (s m t)"),
+            )
+
+        def project(k):
             def mx(acc, s, cols):
                 nc.tensor.matmul_mx(
                     out=acc,
-                    lhsT=o_codes[:, tile_index, s * P : (s + 1) * P].bitcast(FP8X4),
-                    lhsT_scale=o_scales[:, tile_index, s * P : (s + 1) * P],
+                    lhsT=o_codes[:, k, s * P : (s + 1) * P].bitcast(FP8X4),
+                    lhsT_scale=o_scales[:, k, s * P : (s + 1) * P],
                     rhs=w_codes[:, cols].bitcast(FP8X4),
                     rhs_scale=w_scales[:, cols],
                     start=True,
@@ -149,45 +173,89 @@ def tile_multiheadattention_pa_kernel(tc, attn_out, inp, w_proj1, w_proj2, ln_a,
             mx(y0[:], 0, slice(0, BANK))
             mx(y1[:, 0 : N1 - BANK], 0, slice(BANK, N1))
             mx(y1[:, N1 - BANK : BANK], 1, slice(N1, D_MODEL))
-            return [y0, y1]
+            y[k] = [y0, y1]
 
-        def norm(g, r, y):
-            z = work.tile([P, D_MODEL], F32)
-            sums = small.tile([P, 2], F32)
+        def add_residual(k):
+            z_k = work.tile([P, D_MODEL], F32, name="z")
+            sums_k = small.tile([P, 2], F32, name="sums")
             for c in range(2):
                 cols = slice(c * BANK, (c + 1) * BANK)
                 nc.vector.scalar_tensor_tensor(
-                    out=z[:, cols], in0=y[c][:], scalar=1.0, in1=inp_sb[g][:, r, cols],
-                    op0=ALU.mult, op1=ALU.add, accum_out=sums[:, c : c + 1],
+                    out=z_k[:, cols], in0=y[k][c][:], scalar=1.0, in1=inp_sb[k // ROWS][:, k % ROWS, cols],
+                    op0=ALU.mult, op1=ALU.add, accum_out=sums_k[:, c : c + 1],
                 )
-            neg_mean = small.tile([P, 1], F32)
+            z[k] = z_k
+            sums[k] = sums_k
+
+        def mean(k):
+            neg = small.tile([P, 1], F32, name="neg_mean")
             nc.vector.tensor_scalar(
-                out=neg_mean[:], in0=sums[:, 0:1], scalar1=sums[:, 1:2], scalar2=-1.0 / D_MODEL, op0=ALU.add, op1=ALU.mult
+                out=neg[:], in0=sums[k][:, 0:1], scalar1=sums[k][:, 1:2], scalar2=-1.0 / D_MODEL, op0=ALU.add, op1=ALU.mult
             )
-            squares = work.tile([P, D_MODEL], BF16)
-            sum_sq = small.tile([P, 1], F32)
-            nc.scalar.activation(out=squares[:], in_=z[:], func=ACT.Square, bias=neg_mean[:], scale=1.0, accum_out=sum_sq[:])
-            sigma = small.tile([P, 1], F32)
-            nc.scalar.activation(out=sigma[:], in_=sum_sq[:], func=ACT.Sqrt, bias=TINY, scale=1.0 / (D_MODEL - 1))
-            gained = work.tile([P, D_MODEL], F32)
-            for c in range(2):
-                cols = slice(c * BANK, (c + 1) * BANK)
-                nc.vector.scalar_tensor_tensor(
-                    out=gained[:, cols], in0=z[:, cols], scalar=neg_mean[:], in1=gain[c][:], op0=ALU.add, op1=ALU.mult
-                )
-            denom = small.tile([P, 1], F32)
-            nc.vector.tensor_scalar_add(out=denom[:], in0=sigma[:], scalar1=EPS)
-            inv = small.tile([P, 1], F32)
-            nc.vector.reciprocal(out=inv[:], in_=denom[:])
-            scaled = work.tile([P, D_MODEL], F32)
-            nc.scalar.activation(out=scaled[:], in_=gained[:], func=ACT.Copy, scale=inv[:])
+            neg_mean[k] = neg
+
+        def squares(k):
+            unused = work.tile([P, D_MODEL], BF16, name="squares")
+            total = small.tile([P, 1], F32, name="sum_sq")
+            nc.scalar.activation(out=unused[:], in_=z[k][:], func=ACT.Square, bias=neg_mean[k][:], scale=1.0, accum_out=total[:])
+            sum_sq[k] = total
+
+        def root(k):
+            sigma_k = small.tile([P, 1], F32, name="sigma")
+            nc.scalar.activation(out=sigma_k[:], in_=sum_sq[k][:], func=ACT.Sqrt, bias=TINY, scale=1.0 / (D_MODEL - 1))
+            sigma[k] = sigma_k
+
+        def apply_gain(k, c):
+            cols = slice(c * BANK, (c + 1) * BANK)
+            nc.vector.scalar_tensor_tensor(
+                out=gained[k][:, cols], in0=z[k][:, cols], scalar=neg_mean[k][:], in1=gain[c][:], op0=ALU.add, op1=ALU.mult
+            )
+
+        def gain_low(k):
+            gained_k = work.tile([P, D_MODEL], F32, name="gained")
+            gained[k] = gained_k
+            apply_gain(k, 0)
+
+        def gain_high(k):
+            apply_gain(k, 1)
+
+        def add_eps(k):
+            denom_k = small.tile([P, 1], F32, name="denom")
+            nc.vector.tensor_scalar_add(out=denom_k[:], in0=sigma[k][:], scalar1=EPS)
+            denom[k] = denom_k
+
+        def invert(k):
+            inv_k = small.tile([P, 1], F32, name="inv")
+            nc.vector.reciprocal(out=inv_k[:], in_=denom[k][:])
+            inv[k] = inv_k
+
+        def finish(k):
+            tail = k >= TILES - TAIL_TILES
+            v_cols = TAIL_V_COLS if tail else 0
+            g_first = D_MODEL if tail else G_FIRST
             result = work.tile([P, D_MODEL], F32)
-            nc.gpsimd.tensor_tensor(out=result[:], in0=scaled[:], in1=bias[:], op=ALU.add)
-            nc.sync.dma_start(out=out_groups[g][:, r, :], in_=result[:])
+            if v_cols > 0:
+                nc.vector.scalar_tensor_tensor(
+                    out=result[:, :v_cols], in0=gained[k][:, :v_cols], scalar=inv[k][:], in1=bias[:, :v_cols],
+                    op0=ALU.mult, op1=ALU.add,
+                )
+            scaled = work.tile([P, D_MODEL], F32)
+            if g_first < D_MODEL:
+                nc.gpsimd.tensor_scalar(
+                    out=scaled[:, g_first:], in0=gained[k][:, g_first:], scalar1=inv[k][:], scalar2=0.0, op0=ALU.mult, op1=ALU.add
+                )
+            nc.scalar.activation(out=scaled[:, v_cols:g_first], in_=gained[k][:, v_cols:g_first], func=ACT.Copy, scale=inv[k][:])
+            nc.gpsimd.tensor_tensor(out=result[:, v_cols:], in0=scaled[:, v_cols:], in1=bias[:, v_cols:], op=ALU.add)
+            nc.sync.dma_start(out=out_groups[k // ROWS][:, k % ROWS, :], in_=result[:])
 
-        quantise_group(0)
-        first = [project(r) for r in range(ROWS)]
-
+        sort_features(0)
+        flip(0)
+        flip(1)
+        evacuate(0)
+        regroup_weight(nc.vector.tensor_copy, N1, w2_raw[:])
+        quantise(0)
+        regroup_weight(nc.vector.tensor_copy, 0, w1_raw[:, :, 0:BANK])
+        regroup_weight(nc.scalar.copy, BANK, w1_raw[:, :, BANK:N1])
         gain = []
         for c in range(2):
             gain_c = gain_psum.tile([P, BANK], F32, name="gain%d" % c)
@@ -195,14 +263,37 @@ def tile_multiheadattention_pa_kernel(tc, attn_out, inp, w_proj1, w_proj2, ln_a,
             gain.append(gain_c)
         bias = keep.tile([P, D_MODEL], F32)
         for c in range(2):
-            bias_c = t_psum.tile([P, BANK], F32, tag="xt")
+            bias_c = y_psum.tile([P, BANK], F32, tag="y%d" % c)
             nc.tensor.matmul(
                 out=bias_c[:], lhsT=ones[:], rhs=rows[:, D_MODEL + c * BANK : D_MODEL + (c + 1) * BANK], start=True, stop=True
             )
             nc.scalar.copy(out=bias[:, c * BANK : (c + 1) * BANK], in_=bias_c[:])
+        evacuate(1)
+        quantise_weight(0)
+        quantise_weight(1)
+        project(0)
+        sort_features(2)
+        quantise(1)
+        flip(2)
+        project(1)
+        evacuate(2)
 
-        for g in range(GROUPS):
-            if g + 1 < GROUPS:
-                quantise_group(g + 1)
-            for r in range(ROWS):
-                norm(g, r, first[r] if g == 0 else project(g * ROWS + r))
+        def at(k, stage_of):
+            if 0 <= k < TILES:
+                stage_of(k)
+
+        for k in range(TILES + 1):
+            at(k, add_residual)
+            at(k - 1, gain_low)
+            at(k, mean)
+            at(k - 1, gain_high)
+            at(k, squares)
+            at(k - 1, add_eps)
+            at(k + 2, quantise)
+            at(k - 1, invert)
+            at(k - 1, finish)
+            at(k, root)
+            at(k + 3, flip)
+            at(k + 3, evacuate)
+            at(k + 2, project)
+            at(k + 4, sort_features)

@@ -54,6 +54,8 @@ def tile_multiheadattention_pa_kernel(tc, attn_out, inp, w_proj1, w_proj2, ln_a,
 
         rows = keep.tile([P, 2 * D_MODEL], BF16)
         nc.vector.memset(rows[:], 0.0)
+        nc.scalar.dma_start(out=rows[0:1, 0:D_MODEL], in_=ln_a.unsqueeze(0))
+        nc.scalar.dma_start(out=rows[0:1, D_MODEL : 2 * D_MODEL], in_=ln_b.unsqueeze(0))
         ones = keep.tile([P, P], BF16)
         nc.vector.memset(ones[:], 1.0)
         one = keep.tile([P, 1], F32)
@@ -77,8 +79,6 @@ def tile_multiheadattention_pa_kernel(tc, attn_out, inp, w_proj1, w_proj2, ln_a,
             inp_sb.append(inp_g)
 
         load_attention(0)
-        nc.sync.dma_start(out=rows[0:1, 0:D_MODEL], in_=ln_a.unsqueeze(0))
-        nc.sync.dma_start(out=rows[0:1, D_MODEL : 2 * D_MODEL], in_=ln_b.unsqueeze(0))
         w2_raw = keep.tile([P, 4, N2], BF16)
         nc.sync.dma_start(
             out=w2_raw[:].rearrange("q (u e) n -> q u (e n)", u=2), in_=w_proj2.rearrange("(u q e) n -> q u (e n)", u=2, e=2)
@@ -256,18 +256,6 @@ def tile_multiheadattention_pa_kernel(tc, attn_out, inp, w_proj1, w_proj2, ln_a,
         quantise(0)
         regroup_weight(nc.vector.tensor_copy, 0, w1_raw[:, :, 0:BANK])
         regroup_weight(nc.scalar.copy, BANK, w1_raw[:, :, BANK:N1])
-        gain = []
-        for c in range(2):
-            gain_c = gain_psum.tile([P, BANK], F32, name="gain%d" % c)
-            nc.tensor.matmul(out=gain_c[:], lhsT=ones[:], rhs=rows[:, c * BANK : (c + 1) * BANK], start=True, stop=True)
-            gain.append(gain_c)
-        bias = keep.tile([P, D_MODEL], F32)
-        for c in range(2):
-            bias_c = y_psum.tile([P, BANK], F32, tag="y%d" % c)
-            nc.tensor.matmul(
-                out=bias_c[:], lhsT=ones[:], rhs=rows[:, D_MODEL + c * BANK : D_MODEL + (c + 1) * BANK], start=True, stop=True
-            )
-            nc.scalar.copy(out=bias[:, c * BANK : (c + 1) * BANK], in_=bias_c[:])
         evacuate(1)
         quantise_weight(0)
         quantise_weight(1)
@@ -277,6 +265,18 @@ def tile_multiheadattention_pa_kernel(tc, attn_out, inp, w_proj1, w_proj2, ln_a,
         flip(2)
         project(1)
         evacuate(2)
+        gain = []
+        for c in range(2):
+            gain_c = gain_psum.tile([P, BANK], F32, name="gain%d" % c)
+            nc.tensor.matmul(out=gain_c[:], lhsT=ones[:], rhs=rows[:, c * BANK : (c + 1) * BANK], start=True, stop=True)
+            gain.append(gain_c)
+        bias = keep.tile([P, D_MODEL], F32)
+        for c in range(2):
+            bias_c = t_psum.tile([P, BANK], F32, tag="xt")
+            nc.tensor.matmul(
+                out=bias_c[:], lhsT=ones[:], rhs=rows[:, D_MODEL + c * BANK : D_MODEL + (c + 1) * BANK], start=True, stop=True
+            )
+            nc.scalar.copy(out=bias[:, c * BANK : (c + 1) * BANK], in_=bias_c[:])
 
         def at(k, stage_of):
             if 0 <= k < TILES:

@@ -23,13 +23,9 @@ D_MODEL = N1 + N2
 BANK = 512
 EPS = 1e-3
 TINY = 1e-30
-
-ROWS = 2
-GROUPS = TOKENS // (P * ROWS)
-TILES = GROUPS * ROWS
+TILES = TOKENS // P
 
 TAIL_TILES = 2
-G_FIRST = 768
 TAIL_V_COLS = 768
 
 FLOPS = 2 * TOKENS * K * D_MODEL
@@ -37,13 +33,13 @@ FLOPS = 2 * TOKENS * K * D_MODEL
 
 def tile_multiheadattention_pa_kernel(tc, attn_out, inp, w_proj1, w_proj2, ln_a, ln_b, out):
     nc = tc.nc
-    attn_groups = attn_out.rearrange("h g (p r) d -> g p h (r d)", r=ROWS)
-    inp_groups = inp.rearrange("(g p r) n -> g p (r n)", g=GROUPS, r=ROWS)
-    out_groups = out.rearrange("(g p r) n -> g p r n", g=GROUPS, r=ROWS)
+    attn_tiles = attn_out.rearrange("h b l d -> h (b l) d").rearrange("h (k p) d -> k p h d", p=P)
+    inp_tiles = inp.rearrange("(k p) n -> k p n", p=P)
+    out_tiles = out.rearrange("(k p) n -> k p n", p=P)
 
     with ExitStack() as ctx:
         keep = ctx.enter_context(tc.tile_pool(name="keep", bufs=1))
-        loads = ctx.enter_context(tc.tile_pool(name="loads", bufs=GROUPS))
+        loads = ctx.enter_context(tc.tile_pool(name="loads", bufs=TILES))
         stage = ctx.enter_context(tc.tile_pool(name="stage", bufs=3))
         work = ctx.enter_context(tc.tile_pool(name="work", bufs=3))
         small = ctx.enter_context(tc.tile_pool(name="small", bufs=4))
@@ -54,8 +50,6 @@ def tile_multiheadattention_pa_kernel(tc, attn_out, inp, w_proj1, w_proj2, ln_a,
 
         rows = keep.tile([P, 2 * D_MODEL], BF16)
         nc.vector.memset(rows[:], 0.0)
-        nc.scalar.dma_start(out=rows[0:1, 0:D_MODEL], in_=ln_a.unsqueeze(0))
-        nc.scalar.dma_start(out=rows[0:1, D_MODEL : 2 * D_MODEL], in_=ln_b.unsqueeze(0))
         ones = keep.tile([P, P], BF16)
         nc.vector.memset(ones[:], 1.0)
         one = keep.tile([P, 1], F32)
@@ -65,20 +59,22 @@ def tile_multiheadattention_pa_kernel(tc, attn_out, inp, w_proj1, w_proj2, ln_a,
         ident = keep.tile([P, P], F32)
         make_identity(nc, ident[:])
 
-        x_raw = []
-        inp_sb = []
+        x_raw = {}
+        inp_sb = {}
 
-        def load_attention(g):
-            x_g = loads.tile([P, HEADS, ROWS * D_V], BF16, name="x_raw")
-            nc.sync.dma_start(out=x_g[:], in_=attn_groups[g])
-            x_raw.append(x_g)
+        def load_attention(k):
+            x_k = loads.tile([P, HEADS, D_V], BF16, name="x_raw")
+            nc.sync.dma_start(out=x_k[:], in_=attn_tiles[k])
+            x_raw[k] = x_k
 
-        def load_residual(g):
-            inp_g = loads.tile([P, ROWS, D_MODEL], BF16, name="inp_sb")
-            nc.sync.dma_start(out=inp_g[:].rearrange("p r n -> p (r n)"), in_=inp_groups[g])
-            inp_sb.append(inp_g)
+        def load_residual(k):
+            inp_k = loads.tile([P, D_MODEL], BF16, name="inp_sb")
+            nc.sync.dma_start(out=inp_k[:], in_=inp_tiles[k])
+            inp_sb[k] = inp_k
 
         load_attention(0)
+        nc.sync.dma_start(out=rows[0:1, 0:D_MODEL], in_=ln_a.unsqueeze(0))
+        nc.sync.dma_start(out=rows[0:1, D_MODEL : 2 * D_MODEL], in_=ln_b.unsqueeze(0))
         w2_raw = keep.tile([P, 4, N2], BF16)
         nc.sync.dma_start(
             out=w2_raw[:].rearrange("q (u e) n -> q u (e n)", u=2), in_=w_proj2.rearrange("(u q e) n -> q u (e n)", u=2, e=2)
@@ -88,9 +84,12 @@ def tile_multiheadattention_pa_kernel(tc, attn_out, inp, w_proj1, w_proj2, ln_a,
             out=w1_raw[:].rearrange("q (u e) n -> q u (e n)", u=2), in_=w_proj1.rearrange("(u q e) n -> q u (e n)", u=2, e=2)
         )
         load_residual(0)
-        for g in range(1, GROUPS):
-            load_attention(g)
-            load_residual(g)
+        load_attention(1)
+        load_attention(2)
+        for k in range(1, TILES):
+            load_residual(k)
+            if k + 2 < TILES:
+                load_attention(k + 2)
 
         w_grouped = keep.tile([P, D_MODEL, 4], BF16, align_bytes=64)
         w_codes = keep.tile([P, D_MODEL], U32, align_bytes=64)
@@ -127,21 +126,19 @@ def tile_multiheadattention_pa_kernel(tc, attn_out, inp, w_proj1, w_proj2, ln_a,
         inv = {}
 
         def sort_features(k):
-            if k % ROWS != 0:
-                return
-            split = stage.tile([P, ROWS, 2, K], BF16, name="x_split")
+            split = stage.tile([P, 2, K], BF16, name="x_split")
             nc.vector.tensor_copy(
-                out=split[:].rearrange("p r s (h j) -> p r s h j", j=HALF),
-                in_=x_raw[k // ROWS][:].rearrange("p h (r s j) -> p r s h j", r=ROWS, s=2),
+                out=split[:].rearrange("p s (h j) -> p s h j", j=HALF),
+                in_=x_raw[k][:].rearrange("p h (s j) -> p s h j", s=2),
             )
-            x_split[k // ROWS] = split
+            x_split[k] = split
 
         def flip(k):
-            words = x_split[k // ROWS][:].bitcast(F32)
+            words = x_split[k][:].bitcast(F32)
             planes = t_psum.tile([P, 2, 2, P], F32, name="xt")
             for s in range(2):
                 for u in range(2):
-                    nc.tensor.transpose(planes[:, s, u, :], words[:, k % ROWS, s, u * P : (u + 1) * P], ident[:])
+                    nc.tensor.transpose(planes[:, s, u, :], words[:, s, u * P : (u + 1) * P], ident[:])
             xt[k] = planes
 
         def evacuate(k):
@@ -181,7 +178,7 @@ def tile_multiheadattention_pa_kernel(tc, attn_out, inp, w_proj1, w_proj2, ln_a,
             for c in range(2):
                 cols = slice(c * BANK, (c + 1) * BANK)
                 nc.vector.scalar_tensor_tensor(
-                    out=z_k[:, cols], in0=y[k][c][:], scalar=1.0, in1=inp_sb[k // ROWS][:, k % ROWS, cols],
+                    out=z_k[:, cols], in0=y[k][c][:], scalar=1.0, in1=inp_sb[k][:, cols],
                     op0=ALU.mult, op1=ALU.add, accum_out=sums_k[:, c : c + 1],
                 )
             z[k] = z_k
@@ -230,9 +227,7 @@ def tile_multiheadattention_pa_kernel(tc, attn_out, inp, w_proj1, w_proj2, ln_a,
             inv[k] = inv_k
 
         def finish(k):
-            tail = k >= TILES - TAIL_TILES
-            v_cols = TAIL_V_COLS if tail else 0
-            g_first = D_MODEL if tail else G_FIRST
+            v_cols = TAIL_V_COLS if k >= TILES - TAIL_TILES else 0
             result = work.tile([P, D_MODEL], F32)
             if v_cols > 0:
                 nc.vector.scalar_tensor_tensor(
@@ -240,31 +235,17 @@ def tile_multiheadattention_pa_kernel(tc, attn_out, inp, w_proj1, w_proj2, ln_a,
                     op0=ALU.mult, op1=ALU.add,
                 )
             scaled = work.tile([P, D_MODEL], F32)
-            if g_first < D_MODEL:
-                nc.gpsimd.tensor_scalar(
-                    out=scaled[:, g_first:], in0=gained[k][:, g_first:], scalar1=inv[k][:], scalar2=0.0, op0=ALU.mult, op1=ALU.add
-                )
-            nc.scalar.activation(out=scaled[:, v_cols:g_first], in_=gained[k][:, v_cols:g_first], func=ACT.Copy, scale=inv[k][:])
+            nc.scalar.activation(out=scaled[:, v_cols:], in_=gained[k][:, v_cols:], func=ACT.Copy, scale=inv[k][:])
             nc.gpsimd.tensor_tensor(out=result[:, v_cols:], in0=scaled[:, v_cols:], in1=bias[:, v_cols:], op=ALU.add)
-            nc.sync.dma_start(out=out_groups[k // ROWS][:, k % ROWS, :], in_=result[:])
+            nc.sync.dma_start(out=out_tiles[k], in_=result[:])
 
         sort_features(0)
         flip(0)
-        flip(1)
         evacuate(0)
         regroup_weight(nc.vector.tensor_copy, N1, w2_raw[:])
         quantise(0)
         regroup_weight(nc.vector.tensor_copy, 0, w1_raw[:, :, 0:BANK])
         regroup_weight(nc.scalar.copy, BANK, w1_raw[:, :, BANK:N1])
-        evacuate(1)
-        quantise_weight(0)
-        quantise_weight(1)
-        project(0)
-        sort_features(2)
-        quantise(1)
-        flip(2)
-        project(1)
-        evacuate(2)
         gain = []
         for c in range(2):
             gain_c = gain_psum.tile([P, BANK], F32, name="gain%d" % c)
@@ -272,28 +253,38 @@ def tile_multiheadattention_pa_kernel(tc, attn_out, inp, w_proj1, w_proj2, ln_a,
             gain.append(gain_c)
         bias = keep.tile([P, D_MODEL], F32)
         for c in range(2):
-            bias_c = t_psum.tile([P, BANK], F32, tag="xt")
+            bias_c = y_psum.tile([P, BANK], F32, tag="y%d" % c)
             nc.tensor.matmul(
                 out=bias_c[:], lhsT=ones[:], rhs=rows[:, D_MODEL + c * BANK : D_MODEL + (c + 1) * BANK], start=True, stop=True
             )
             nc.scalar.copy(out=bias[:, c * BANK : (c + 1) * BANK], in_=bias_c[:])
+        quantise_weight(0)
+        quantise_weight(1)
+        project(0)
+        for k in range(1, 3):
+            sort_features(k)
+            flip(k)
+            evacuate(k)
 
         def at(k, stage_of):
             if 0 <= k < TILES:
                 stage_of(k)
 
+        projected = 1
         for k in range(TILES + 1):
             at(k, add_residual)
-            at(k - 1, gain_low)
+            at(k + 3, sort_features)
             at(k, mean)
-            at(k - 1, gain_high)
             at(k, squares)
+            at(k + 3, flip)
+            while projected <= min(k + 2, TILES - 1):
+                quantise(projected)
+                project(projected)
+                projected += 1
+            at(k, gain_low)
             at(k - 1, add_eps)
-            at(k + 2, quantise)
+            at(k, gain_high)
             at(k - 1, invert)
+            at(k + 3, evacuate)
             at(k - 1, finish)
             at(k, root)
-            at(k + 3, flip)
-            at(k + 3, evacuate)
-            at(k + 2, project)
-            at(k + 4, sort_features)

@@ -73,8 +73,6 @@ def tile_multiheadattention_pa_kernel(tc, attn_out, inp, w_proj1, w_proj2, ln_a,
             inp_sb[k] = inp_k
 
         load_attention(0)
-        nc.sync.dma_start(out=rows[0:1, 0:D_MODEL], in_=ln_a.unsqueeze(0))
-        nc.sync.dma_start(out=rows[0:1, D_MODEL : 2 * D_MODEL], in_=ln_b.unsqueeze(0))
         w2_raw = keep.tile([P, 4, N2], BF16)
         nc.sync.dma_start(
             out=w2_raw[:].rearrange("q (u e) n -> q u (e n)", u=2), in_=w_proj2.rearrange("(u q e) n -> q u (e n)", u=2, e=2)
@@ -83,6 +81,8 @@ def tile_multiheadattention_pa_kernel(tc, attn_out, inp, w_proj1, w_proj2, ln_a,
         nc.sync.dma_start(
             out=w1_raw[:].rearrange("q (u e) n -> q u (e n)", u=2), in_=w_proj1.rearrange("(u q e) n -> q u (e n)", u=2, e=2)
         )
+        nc.sync.dma_start(out=rows[0:1, 0:D_MODEL], in_=ln_a.unsqueeze(0))
+        nc.sync.dma_start(out=rows[0:1, D_MODEL : 2 * D_MODEL], in_=ln_b.unsqueeze(0))
         load_residual(0)
         load_attention(1)
         load_attention(2)
@@ -124,6 +124,7 @@ def tile_multiheadattention_pa_kernel(tc, attn_out, inp, w_proj1, w_proj2, ln_a,
         gained = {}
         denom = {}
         inv = {}
+        result = {}
 
         def sort_features(k):
             split = stage.tile([P, 2, K], BF16, name="x_split")
@@ -172,17 +173,22 @@ def tile_multiheadattention_pa_kernel(tc, attn_out, inp, w_proj1, w_proj2, ln_a,
             mx(y1[:, N1 - BANK : BANK], 1, slice(N1, D_MODEL))
             y[k] = [y0, y1]
 
-        def add_residual(k):
+        def add_residual(k, c):
+            cols = slice(c * BANK, (c + 1) * BANK)
+            nc.vector.scalar_tensor_tensor(
+                out=z[k][:, cols], in0=y[k][c][:], scalar=1.0, in1=inp_sb[k][:, cols],
+                op0=ALU.mult, op1=ALU.add, accum_out=sums[k][:, c : c + 1],
+            )
+
+        def residual_low(k):
             z_k = work.tile([P, D_MODEL], F32, name="z")
             sums_k = small.tile([P, 2], F32, name="sums")
-            for c in range(2):
-                cols = slice(c * BANK, (c + 1) * BANK)
-                nc.vector.scalar_tensor_tensor(
-                    out=z_k[:, cols], in0=y[k][c][:], scalar=1.0, in1=inp_sb[k][:, cols],
-                    op0=ALU.mult, op1=ALU.add, accum_out=sums_k[:, c : c + 1],
-                )
             z[k] = z_k
             sums[k] = sums_k
+            add_residual(k, 0)
+
+        def residual_high(k):
+            add_residual(k, 1)
 
         def mean(k):
             neg = small.tile([P, 1], F32, name="neg_mean")
@@ -226,18 +232,25 @@ def tile_multiheadattention_pa_kernel(tc, attn_out, inp, w_proj1, w_proj2, ln_a,
             nc.vector.reciprocal(out=inv_k[:], in_=denom[k][:])
             inv[k] = inv_k
 
-        def finish(k):
-            v_cols = TAIL_V_COLS if k >= TILES - TAIL_TILES else 0
-            result = work.tile([P, D_MODEL], F32)
+        def vector_cols(k):
+            return TAIL_V_COLS if k >= TILES - TAIL_TILES else 0
+
+        def finish_on_vector(k):
+            result_k = work.tile([P, D_MODEL], F32, name="result")
+            result[k] = result_k
+            v_cols = vector_cols(k)
             if v_cols > 0:
                 nc.vector.scalar_tensor_tensor(
-                    out=result[:, :v_cols], in0=gained[k][:, :v_cols], scalar=inv[k][:], in1=bias[:, :v_cols],
+                    out=result_k[:, :v_cols], in0=gained[k][:, :v_cols], scalar=inv[k][:], in1=bias[:, :v_cols],
                     op0=ALU.mult, op1=ALU.add,
                 )
+
+        def finish(k):
+            v_cols = vector_cols(k)
             scaled = work.tile([P, D_MODEL], F32)
             nc.scalar.activation(out=scaled[:, v_cols:], in_=gained[k][:, v_cols:], func=ACT.Copy, scale=inv[k][:])
-            nc.gpsimd.tensor_tensor(out=result[:, v_cols:], in0=scaled[:, v_cols:], in1=bias[:, v_cols:], op=ALU.add)
-            nc.sync.dma_start(out=out_tiles[k], in_=result[:])
+            nc.gpsimd.tensor_tensor(out=result[k][:, v_cols:], in0=scaled[:, v_cols:], in1=bias[:, v_cols:], op=ALU.add)
+            nc.sync.dma_start(out=out_tiles[k], in_=result[k][:])
 
         sort_features(0)
         flip(0)
@@ -272,19 +285,21 @@ def tile_multiheadattention_pa_kernel(tc, attn_out, inp, w_proj1, w_proj2, ln_a,
 
         projected = 1
         for k in range(TILES + 1):
-            at(k, add_residual)
+            at(k, residual_low)
+            at(k - 1, add_eps)
+            at(k, residual_high)
+            at(k - 1, invert)
             at(k + 3, sort_features)
             at(k, mean)
             at(k, squares)
+            at(k, root)
+            at(k - 1, finish_on_vector)
             at(k + 3, flip)
             while projected <= min(k + 2, TILES - 1):
                 quantise(projected)
                 project(projected)
                 projected += 1
             at(k, gain_low)
-            at(k - 1, add_eps)
             at(k, gain_high)
-            at(k - 1, invert)
             at(k + 3, evacuate)
             at(k - 1, finish)
-            at(k, root)

@@ -124,7 +124,6 @@ def tile_multiheadattention_pa_kernel(tc, attn_out, inp, w_proj1, w_proj2, ln_a,
         gained = {}
         denom = {}
         inv = {}
-        result = {}
 
         def sort_features(k):
             split = stage.tile([P, 2, K], BF16, name="x_split")
@@ -173,22 +172,17 @@ def tile_multiheadattention_pa_kernel(tc, attn_out, inp, w_proj1, w_proj2, ln_a,
             mx(y1[:, N1 - BANK : BANK], 1, slice(N1, D_MODEL))
             y[k] = [y0, y1]
 
-        def add_residual(k, c):
-            cols = slice(c * BANK, (c + 1) * BANK)
-            nc.vector.scalar_tensor_tensor(
-                out=z[k][:, cols], in0=y[k][c][:], scalar=1.0, in1=inp_sb[k][:, cols],
-                op0=ALU.mult, op1=ALU.add, accum_out=sums[k][:, c : c + 1],
-            )
-
-        def residual_low(k):
+        def add_residual(k):
             z_k = work.tile([P, D_MODEL], F32, name="z")
             sums_k = small.tile([P, 2], F32, name="sums")
+            for c in range(2):
+                cols = slice(c * BANK, (c + 1) * BANK)
+                nc.vector.scalar_tensor_tensor(
+                    out=z_k[:, cols], in0=y[k][c][:], scalar=1.0, in1=inp_sb[k][:, cols],
+                    op0=ALU.mult, op1=ALU.add, accum_out=sums_k[:, c : c + 1],
+                )
             z[k] = z_k
             sums[k] = sums_k
-            add_residual(k, 0)
-
-        def residual_high(k):
-            add_residual(k, 1)
 
         def mean(k):
             neg = small.tile([P, 1], F32, name="neg_mean")
@@ -232,25 +226,18 @@ def tile_multiheadattention_pa_kernel(tc, attn_out, inp, w_proj1, w_proj2, ln_a,
             nc.vector.reciprocal(out=inv_k[:], in_=denom[k][:])
             inv[k] = inv_k
 
-        def vector_cols(k):
-            return TAIL_V_COLS if k >= TILES - TAIL_TILES else 0
-
-        def finish_on_vector(k):
-            result_k = work.tile([P, D_MODEL], F32, name="result")
-            result[k] = result_k
-            v_cols = vector_cols(k)
+        def finish(k):
+            v_cols = TAIL_V_COLS if k >= TILES - TAIL_TILES else 0
+            result = work.tile([P, D_MODEL], F32)
             if v_cols > 0:
                 nc.vector.scalar_tensor_tensor(
-                    out=result_k[:, :v_cols], in0=gained[k][:, :v_cols], scalar=inv[k][:], in1=bias[:, :v_cols],
+                    out=result[:, :v_cols], in0=gained[k][:, :v_cols], scalar=inv[k][:], in1=bias[:, :v_cols],
                     op0=ALU.mult, op1=ALU.add,
                 )
-
-        def finish(k):
-            v_cols = vector_cols(k)
             scaled = work.tile([P, D_MODEL], F32)
             nc.scalar.activation(out=scaled[:, v_cols:], in_=gained[k][:, v_cols:], func=ACT.Copy, scale=inv[k][:])
-            nc.gpsimd.tensor_tensor(out=result[k][:, v_cols:], in0=scaled[:, v_cols:], in1=bias[:, v_cols:], op=ALU.add)
-            nc.sync.dma_start(out=out_tiles[k], in_=result[k][:])
+            nc.gpsimd.tensor_tensor(out=result[:, v_cols:], in0=scaled[:, v_cols:], in1=bias[:, v_cols:], op=ALU.add)
+            nc.sync.dma_start(out=out_tiles[k], in_=result[:])
 
         sort_features(0)
         flip(0)
@@ -285,21 +272,19 @@ def tile_multiheadattention_pa_kernel(tc, attn_out, inp, w_proj1, w_proj2, ln_a,
 
         projected = 1
         for k in range(TILES + 1):
-            at(k, residual_low)
-            at(k - 1, add_eps)
-            at(k, residual_high)
-            at(k - 1, invert)
+            at(k, add_residual)
             at(k + 3, sort_features)
             at(k, mean)
             at(k, squares)
-            at(k, root)
-            at(k - 1, finish_on_vector)
             at(k + 3, flip)
             while projected <= min(k + 2, TILES - 1):
                 quantise(projected)
                 project(projected)
                 projected += 1
             at(k, gain_low)
+            at(k - 1, add_eps)
             at(k, gain_high)
+            at(k - 1, invert)
             at(k + 3, evacuate)
+            at(k, root)
             at(k - 1, finish)

from contextlib import ExitStack

import concourse.mybir as mybir
from concourse.masks import make_identity

F32 = mybir.dt.float32
BF16 = mybir.dt.bfloat16
U32 = mybir.dt.uint32
U8 = mybir.dt.uint8
FP8X4 = mybir.dt.float8_e4m3fn_x4
ALU = mybir.AluOpType
ACT = mybir.ActivationFunctionType

P = 128
HEADS = 8
D_V = 128
HALF = D_V // 2
TOKENS = 1024
K = HEADS * HALF
N1 = 768
N2 = 256
D_MODEL = N1 + N2
BANK = 512
EPS = 1e-3
TINY = 1e-30
TILES = TOKENS // P

TAIL_TILES = 2
TAIL_V_COLS = 768

FLOPS = 2 * TOKENS * K * D_MODEL


def tile_multiheadattention_pa_kernel(tc, attn_out, inp, w_proj1, w_proj2, ln_a, ln_b, out):
    nc = tc.nc
    attn_tiles = attn_out.rearrange("h b l d -> h (b l) d").rearrange("h (k p) d -> k p h d", p=P)
    inp_tiles = inp.rearrange("(k p) n -> k p n", p=P)
    out_tiles = out.rearrange("(k p) n -> k p n", p=P)

    with ExitStack() as ctx:
        keep = ctx.enter_context(tc.tile_pool(name="keep", bufs=1))
        loads = ctx.enter_context(tc.tile_pool(name="loads", bufs=TILES))
        stage = ctx.enter_context(tc.tile_pool(name="stage", bufs=3))
        work = ctx.enter_context(tc.tile_pool(name="work", bufs=3))
        small = ctx.enter_context(tc.tile_pool(name="small", bufs=4))
        gain_psum = ctx.enter_context(tc.psum_pool(name="gain_psum", bufs=1))
        y_psum = ctx.enter_context(tc.psum_pool(name="y_psum", bufs=2))
        t_psum = ctx.enter_context(tc.psum_pool(name="t_psum", bufs=2))
        ctx.enter_context(tc.manual_schedule())

        rows = keep.tile([P, 2 * D_MODEL], BF16)
        nc.vector.memset(rows[:], 0.0)
        ones = keep.tile([P, P], BF16)
        nc.vector.memset(ones[:], 1.0)
        one = keep.tile([P, 1], F32)
        nc.vector.memset(one[:], 1.0)
        warm = keep.tile([P, 1], F32)
        nc.scalar.activation(out=warm[:], in_=one[:], func=ACT.Sqrt)
        ident = keep.tile([P, P], F32)
        make_identity(nc, ident[:])

        x_raw = {}
        inp_sb = {}

        def load_attention(k):
            x_k = loads.tile([P, HEADS, D_V], BF16, name="x_raw")
            nc.sync.dma_start(out=x_k[:], in_=attn_tiles[k])
            x_raw[k] = x_k

        def load_residual(k):
            inp_k = loads.tile([P, D_MODEL], BF16, name="inp_sb")
            nc.sync.dma_start(out=inp_k[:], in_=inp_tiles[k])
            inp_sb[k] = inp_k

        load_attention(0)
        w2_raw = keep.tile([P, 4, N2], BF16)
        nc.sync.dma_start(
            out=w2_raw[:].rearrange("q (u e) n -> q u (e n)", u=2), in_=w_proj2.rearrange("(u q e) n -> q u (e n)", u=2, e=2)
        )
        w1_raw = keep.tile([P, 4, N1], BF16)
        nc.sync.dma_start(
            out=w1_raw[:].rearrange("q (u e) n -> q u (e n)", u=2), in_=w_proj1.rearrange("(u q e) n -> q u (e n)", u=2, e=2)
        )
        nc.sync.dma_start(out=rows[0:1, 0:D_MODEL], in_=ln_a.unsqueeze(0))
        nc.sync.dma_start(out=rows[0:1, D_MODEL : 2 * D_MODEL], in_=ln_b.unsqueeze(0))
        load_residual(0)
        load_attention(1)
        load_attention(2)
        for k in range(1, TILES):
            load_residual(k)
            if k + 2 < TILES:
                load_attention(k + 2)

        w_grouped = keep.tile([P, D_MODEL, 4], BF16, align_bytes=64)
        w_codes = keep.tile([P, D_MODEL], U32, align_bytes=64)
        w_scales = keep.tile([P, D_MODEL], U8, align_bytes=64)

        def regroup_weight(copy, first, raw_cols):
            width = raw_cols.shape[2]
            copy(
                out=w_grouped[:, first : first + width, :].rearrange("p (c i) t -> p c t i", i=4),
                in_=raw_cols.rearrange("p t (c i) -> p c t i", i=4),
            )

        def quantise_weight(c):
            cols = slice(c * BANK, (c + 1) * BANK)
            nc.vector.quantize_mx(
                out=w_codes[:, cols].bitcast(FP8X4),
                scales=w_scales[:, cols],
                in_=w_grouped[:, cols, :].rearrange("p n t -> p (n t)"),
            )

        o_codes = keep.tile([P, TILES, 2 * P], U32, align_bytes=64)
        o_scales = keep.tile([P, TILES, 2 * P], U8, align_bytes=64)
        x_split = {}
        xt = {}
        grouped = {}
        y = {}
        z = {}
        sums = {}
        neg_mean = {}
        sum_sq = {}
        sigma = {}
        gained = {}
        denom = {}
        inv = {}

        def sort_features(k):
            split = stage.tile([P, 2, K], BF16, name="x_split")
            nc.vector.tensor_copy(
                out=split[:].rearrange("p s (h j) -> p s h j", j=HALF),
                in_=x_raw[k][:].rearrange("p h (s j) -> p s h j", s=2),
            )
            x_split[k] = split

        def flip(k):
            words = x_split[k][:].bitcast(F32)
            planes = t_psum.tile([P, 2, 2, P], F32, name="xt")
            for s in range(2):
                for u in range(2):
                    nc.tensor.transpose(planes[:, s, u, :], words[:, s, u * P : (u + 1) * P], ident[:])
            xt[k] = planes

        def evacuate(k):
            packed = stage.tile([P, 2, P, 4], BF16, align_bytes=64, name="grouped")
            nc.scalar.copy(out=packed[:].bitcast(F32), in_=xt[k][:].rearrange("p s u m -> p s m u"))
            grouped[k] = packed

        def quantise(k):
            nc.vector.quantize_mx(
                out=o_codes[:, k, :].bitcast(FP8X4),
                scales=o_scales[:, k, :],
                in_=grouped[k][:].rearrange("p s m t -> p (s m t)"),
            )

        def project(k):
            def mx(acc, s, cols):
                nc.tensor.matmul_mx(
                    out=acc,
                    lhsT=o_codes[:, k, s * P : (s + 1) * P].bitcast(FP8X4),
                    lhsT_scale=o_scales[:, k, s * P : (s + 1) * P],
                    rhs=w_codes[:, cols].bitcast(FP8X4),
                    rhs_scale=w_scales[:, cols],
                    start=True,
                    stop=True,
                )

            y0 = y_psum.tile([P, BANK], F32)
            y1 = y_psum.tile([P, BANK], F32)
            mx(y0[:], 0, slice(0, BANK))
            mx(y1[:, 0 : N1 - BANK], 0, slice(BANK, N1))
            mx(y1[:, N1 - BANK : BANK], 1, slice(N1, D_MODEL))
            y[k] = [y0, y1]

        def add_residual(k):
            z_k = work.tile([P, D_MODEL], F32, name="z")
            sums_k = small.tile([P, 2], F32, name="sums")
            for c in range(2):
                cols = slice(c * BANK, (c + 1) * BANK)
                nc.vector.scalar_tensor_tensor(
                    out=z_k[:, cols], in0=y[k][c][:], scalar=1.0, in1=inp_sb[k][:, cols],
                    op0=ALU.mult, op1=ALU.add, accum_out=sums_k[:, c : c + 1],
                )
            z[k] = z_k
            sums[k] = sums_k

        def mean(k):
            neg = small.tile([P, 1], F32, name="neg_mean")
            nc.vector.tensor_scalar(
                out=neg[:], in0=sums[k][:, 0:1], scalar1=sums[k][:, 1:2], scalar2=-1.0 / D_MODEL, op0=ALU.add, op1=ALU.mult
            )
            neg_mean[k] = neg

        def squares(k):
            unused = work.tile([P, D_MODEL], BF16, name="squares")
            total = small.tile([P, 1], F32, name="sum_sq")
            nc.scalar.activation(out=unused[:], in_=z[k][:], func=ACT.Square, bias=neg_mean[k][:], scale=1.0, accum_out=total[:])
            sum_sq[k] = total

        def root(k):
            sigma_k = small.tile([P, 1], F32, name="sigma")
            nc.scalar.activation(out=sigma_k[:], in_=sum_sq[k][:], func=ACT.Sqrt, bias=TINY, scale=1.0 / (D_MODEL - 1))
            sigma[k] = sigma_k

        def apply_gain(k, c):
            cols = slice(c * BANK, (c + 1) * BANK)
            nc.vector.scalar_tensor_tensor(
                out=gained[k][:, cols], in0=z[k][:, cols], scalar=neg_mean[k][:], in1=gain[c][:], op0=ALU.add, op1=ALU.mult
            )

        def gain_low(k):
            gained_k = work.tile([P, D_MODEL], F32, name="gained")
            gained[k] = gained_k
            apply_gain(k, 0)

        def gain_high(k):
            apply_gain(k, 1)

        def add_eps(k):
            denom_k = small.tile([P, 1], F32, name="denom")
            nc.vector.tensor_scalar_add(out=denom_k[:], in0=sigma[k][:], scalar1=EPS)
            denom[k] = denom_k

        def invert(k):
            inv_k = small.tile([P, 1], F32, name="inv")
            nc.vector.reciprocal(out=inv_k[:], in_=denom[k][:])
            inv[k] = inv_k

        def finish(k):
            v_cols = TAIL_V_COLS if k >= TILES - TAIL_TILES else 0
            result = work.tile([P, D_MODEL], F32)
            if v_cols > 0:
                nc.vector.scalar_tensor_tensor(
                    out=result[:, :v_cols], in0=gained[k][:, :v_cols], scalar=inv[k][:], in1=bias[:, :v_cols],
                    op0=ALU.mult, op1=ALU.add,
                )
            scaled = work.tile([P, D_MODEL], F32)
            nc.scalar.activation(out=scaled[:, v_cols:], in_=gained[k][:, v_cols:], func=ACT.Copy, scale=inv[k][:])
            nc.gpsimd.tensor_tensor(out=result[:, v_cols:], in0=scaled[:, v_cols:], in1=bias[:, v_cols:], op=ALU.add)
            nc.sync.dma_start(out=out_tiles[k], in_=result[:])

        sort_features(0)
        flip(0)
        evacuate(0)
        regroup_weight(nc.vector.tensor_copy, N1, w2_raw[:])
        quantise(0)
        regroup_weight(nc.vector.tensor_copy, 0, w1_raw[:, :, 0:BANK])
        regroup_weight(nc.scalar.copy, BANK, w1_raw[:, :, BANK:N1])
        gain = []
        for c in range(2):
            gain_c = gain_psum.tile([P, BANK], F32, name="gain%d" % c)
            nc.tensor.matmul(out=gain_c[:], lhsT=ones[:], rhs=rows[:, c * BANK : (c + 1) * BANK], start=True, stop=True)
            gain.append(gain_c)
        bias = keep.tile([P, D_MODEL], F32)
        for c in range(2):
            bias_c = y_psum.tile([P, BANK], F32, tag="y%d" % c)
            nc.tensor.matmul(
                out=bias_c[:], lhsT=ones[:], rhs=rows[:, D_MODEL + c * BANK : D_MODEL + (c + 1) * BANK], start=True, stop=True
            )
            nc.scalar.copy(out=bias[:, c * BANK : (c + 1) * BANK], in_=bias_c[:])
        quantise_weight(0)
        quantise_weight(1)
        project(0)
        for k in range(1, 3):
            sort_features(k)
            flip(k)
            evacuate(k)

        def at(k, stage_of):
            if 0 <= k < TILES:
                stage_of(k)

        projected = 1
        for k in range(TILES + 1):
            at(k, add_residual)
            at(k + 3, sort_features)
            at(k, mean)
            at(k, squares)
            at(k + 3, flip)
            while projected <= min(k + 2, TILES - 1):
                quantise(projected)
                project(projected)
                projected += 1
            at(k, gain_low)
            at(k - 1, add_eps)
            at(k, gain_high)
            at(k - 1, invert)
            at(k + 3, evacuate)
            at(k, root)
            at(k - 1, finish)
